import numpy as np
import ml_dtypes


def mxq(x, axis, fmt="e4m3"):
    dtype, down = {"e4m3": (ml_dtypes.float8_e4m3fn, 7), "e5m2": (ml_dtypes.float8_e5m2, 14)}[fmt]
    v = np.moveaxis(np.asarray(x, np.float32).astype(ml_dtypes.bfloat16).astype(np.float64), axis, -1)
    blocks = v.reshape(v.shape[:-1] + (-1, 32))
    amax = np.abs(blocks).max(-1, keepdims=True)
    byte = np.maximum(np.where(amax > 0, np.frexp(amax)[1] - 1 + 127, 0) - down, 1)
    scale = np.exp2(byte - 127.0)
    codes = (blocks / scale).astype(np.float32).astype(dtype).astype(np.float64)
    return np.moveaxis((codes * scale).reshape(v.shape), -1, axis)


WIDE = False


def mx_kscale(k):
    if not WIDE:
        return np.ones(k)
    levels = np.array([10, -10, 5, -5, 0])
    if k % 512:
        return np.exp2(np.random.permutation(np.resize(levels, k // 32))).repeat(32)
    a = np.empty((k // 512, 16))
    for p in range(k // 512):
        a[p, :8] = np.random.permutation(np.resize(levels, 8))
        for g in range(8):
            far = levels[np.abs(levels - a[p, g]) >= 10]
            a[p, g + 8] = far[np.random.randint(len(far))]
    return np.exp2(a.ravel()).repeat(32)


BF16 = ml_dtypes.bfloat16


def bf(x):
    return np.asarray(x, np.float32).astype(BF16)


def f64(x):
    return np.asarray(x).astype(np.float64)


B, D_IN, H, D_OUT = 512, 4096, 2048, 1024
H2 = 2 * H
LN_EPS = 1e-5


def setup_inputs():
    s = mx_kscale(H)
    t = mx_kscale(H2)
    return {
        "h1": bf(np.tanh(np.random.standard_normal((B, H))) * s),
        "W_ih1": bf(np.random.standard_normal((H, H)) / np.sqrt(H) / s[None, :]),
        "b_ih1": bf(0.25 + 0.3 * np.random.standard_normal(H)),
        "b_hh1": bf(0.3 * np.random.standard_normal(H)),
        "ln_g": bf((1.0 + 0.1 * np.random.standard_normal(H2)) * t),
        "ln_b": bf(0.2 * np.random.standard_normal(H2) * t),
        "fc_W": bf(np.random.standard_normal((D_OUT, H2)) / np.sqrt(H2) / t[None, :]),
        "fc_b": bf(0.3 * np.random.standard_normal(D_OUT)),
    }


def reference(h1, W_ih1, b_ih1, b_hh1, ln_g, ln_b, fc_W, fc_b):
    h2 = np.tanh((mxq(f64(h1), 1, "e4m3") @ mxq(f64(W_ih1), 1, "e4m3").T) + f64(b_ih1) + f64(b_hh1))
    combined = np.concatenate([h2, h2], axis=1)
    mu = combined.mean(axis=-1, keepdims=True)
    var = combined.var(axis=-1, keepdims=True)
    normed = (combined - mu) / np.sqrt(var + LN_EPS) * f64(ln_g) + f64(ln_b)
    return (mxq(normed, 1, "e4m3") @ mxq(f64(fc_W), 1, "e4m3").T) + f64(fc_b)

@@ -1,0 +1,347 @@
+from contextlib import ExitStack
+
+import concourse.mybir as mybir
+from concourse.masks import make_identity
+
+F32 = mybir.dt.float32
+BF16 = mybir.dt.bfloat16
+U32 = mybir.dt.uint32
+U8 = mybir.dt.uint8
+FP8X4 = mybir.dt.float8_e4m3fn_x4
+ALU = mybir.AluOpType
+ACT = mybir.ActivationFunctionType
+
+P = 128
+B, H, D_OUT = 512, 2048, 1024
+LN_EPS = 1e-5
+FLOPS = 2 * B * H * H + 2 * B * 2 * H * D_OUT
+
+
+N0 = (10, 17)
+RG_LAG = (3, 4)
+MM_LAG = (4, 5)
+N_STEPS = 29
+
+
+def tile_rnnclassifier_pa_kernel(tc, h1, W_ih1, b_ih1, b_hh1, ln_g, ln_b, fc_W, fc_b, out):
+    nc = tc.nc
+    with ExitStack() as ctx:
+        const = ctx.enter_context(tc.tile_pool(name="const", bufs=1))
+        rawp = ctx.enter_context(tc.tile_pool(name="raw", bufs=4))
+        grpp = ctx.enter_context(tc.tile_pool(name="grouped", bufs=3))
+        wfp = ctx.enter_context(tc.tile_pool(name="wfcodes", bufs=10))
+        plp = ctx.enter_context(tc.tile_pool(name="planes", bufs=4))
+        gnp = ctx.enter_context(tc.tile_pool(name="gnorm", bufs=3))
+        osp = ctx.enter_context(tc.tile_pool(name="outs", bufs=4))
+        psp = ctx.enter_context(tc.psum_pool(name="psum", bufs=8))
+        ctx.enter_context(tc.manual_schedule())
+
+        def bank(name):
+            return psp.tile([P, 512], F32, name=name, tag="ps")
+
+        def slab_off(pos, i, a, u):
+            if pos == 0 or pos == 9:
+                return (i // 2) * 1024 + (2 * (i % 2) + a) * 256 + u
+            if pos < 9:
+                return a * 1024 + i * 256 + u
+            return (2 * i + a) * 256 + u
+
+        raws = {}
+        banks = {}
+        groupeds = {}
+        codes = {}
+        scales = {}
+        loaded = []
+
+        def load():
+            pos = len(loaded)
+            if pos >= 18:
+                return
+            loaded.append(pos)
+            raw = rawp.tile([P, 4096], BF16, name="raw", tag="raw")
+            raws[pos] = raw
+            if pos == 0:
+                for i in range(4):
+                    nc.sync.dma_start(
+                        out=raw[:, i * 1024:(i + 1) * 1024],
+                        in_=h1[(i // 2) * 128:(i // 2 + 1) * 128, (i % 2) * 1024:(i % 2 + 1) * 1024],
+                    )
+            elif pos == 9:
+                nc.sync.dma_start(out=raw[:].rearrange("p (t k) -> p t k", t=2),
+                                  in_=h1[256:512, :].rearrange("(t p) k -> p t k", p=P))
+            elif pos < 9:
+                s = pos - 1
+                nc.sync.dma_start(out=raw[:], in_=W_ih1[(s // 2) * 512:(s // 2 + 1) * 512, :].rearrange("(q v e) k -> q v (e k)", v=2, e=2)[:, s % 2, :])
+            else:
+                f = pos - 10
+                kp = 4 * (f % 2) + f // 2
+                nc.sync.dma_start(
+                    out=raw[:].rearrange("p (c k) -> p c k", c=8),
+                    in_=fc_W[:, kp * 512:(kp + 1) * 512].rearrange("(c p) k -> p c k", p=P),
+                )
+
+        def T(pos):
+            if pos >= 18:
+                return
+            raw_w = raws[pos][:].bitcast(F32)
+            banks[pos] = []
+            for i in range(4):
+                xt = bank("xt")
+                for a in range(2):
+                    for u in range(2):
+                        o = slab_off(pos, i, a, u)
+                        j = 2 * a + u
+                        nc.tensor.transpose(xt[:, j * 128:(j + 1) * 128], raw_w[:, o:o + 255:2], ident[:])
+                banks[pos].append(xt)
+            load()
+
+        def C(pos, vector_share):
+            if pos >= 18:
+                return
+            grouped = grpp.tile([P, 4096], BF16, name="grouped", tag="grouped", align_bytes=64)
+            gw = grouped[:].bitcast(F32)
+            for i in range(4):
+                dst = gw[:, i * 512:(i + 1) * 512].rearrange("p (a c u) -> p a c u", a=2, u=2)
+                src = banks[pos][i][:].rearrange("p (a u c) -> p a c u", a=2, u=2)
+                if i >= 4 - vector_share:
+                    nc.vector.tensor_copy(out=dst, in_=src)
+                else:
+                    nc.scalar.copy(out=dst, in_=src)
+            groupeds[pos] = grouped
+
+        def Q(pos):
+            if pos >= 18:
+                return
+            if pos == 0 or pos == 9:
+                cd = const.tile([P, 1024], U32, name="hcd%d" % pos, align_bytes=64)
+                sc = const.tile([P, 1024], U8, name="hsc%d" % pos, align_bytes=64)
+            else:
+                cd = wfp.tile([P, 1024], U32, name="cd", tag="cd", align_bytes=64)
+                sc = wfp.tile([P, 1024], U8, name="sc", tag="sc", align_bytes=64)
+            nc.vector.quantize_mx(out=cd[:].bitcast(FP8X4), scales=sc[:], in_=groupeds[pos][:])
+            codes[pos] = cd
+            scales[pos] = sc
+
+        for i in range(4):
+            load()
+
+        ident = const.tile([P, P], F32, name="ident")
+        make_identity(nc, ident[:])
+        ones = const.tile([P, P], BF16, name="ones")
+        nc.vector.memset(ones[:], 1.0)
+        brow = const.tile([P, 3072], BF16, name="brow")
+        nc.vector.memset(brow[:], 0.0)
+        gl = const.tile([P, 512], BF16, name="gl")
+        nc.vector.memset(gl[:], 0.0)
+        mhalf = const.tile([P, 4], F32, name="mhalf")
+        nc.vector.memset(mhalf[:], -0.5)
+        warm = const.tile([P, 1], F32, name="warm")
+        nc.vector.memset(warm[:], 0.0)
+        nc.scalar.dma_start(out=brow[0:1, 0:2048], in_=b_ih1.rearrange("(o n) -> o n", o=1))
+        nc.scalar.dma_start(out=brow[1:2, 0:2048], in_=b_hh1.rearrange("(o n) -> o n", o=1))
+        nc.scalar.dma_start(out=brow[0:1, 2048:3072], in_=fc_b.rearrange("(o n) -> o n", o=1))
+        nc.scalar.dma_start(out=gl[0:8, :], in_=ln_g.rearrange("(r c) -> r c", c=512))
+        nc.scalar.dma_start(out=gl[8:16, :], in_=ln_b.rearrange("(r c) -> r c", c=512))
+        nc.scalar.activation(out=warm[:], in_=warm[:], func=ACT.Tanh)
+
+        bias1 = const.tile([P, 2048], F32, name="bias1")
+        fcb = const.tile([P, 1024], F32, name="fcb")
+        gb = const.tile([P, 64], F32, name="gb")
+
+        def BM(c):
+            bp = bank("bp")
+            nc.tensor.matmul(out=bp[:], lhsT=ones[:], rhs=brow[:, c * 512:(c + 1) * 512], start=True, stop=True)
+            if c < 4:
+                nc.vector.tensor_copy(
+                    out=bias1[:, c * 512:(c + 1) * 512].rearrange("p (t q) -> p t q", t=4),
+                    in_=bp[:].rearrange("p (q t) -> p t q", t=4),
+                )
+            else:
+                nc.vector.tensor_copy(out=fcb[:, (c - 4) * 512:(c - 3) * 512], in_=bp[:])
+
+        def GT():
+            gps = bank("gps")
+            for u in range(2):
+                nc.tensor.transpose(gps[:, u * 128:(u + 1) * 128], gl[:].bitcast(F32)[:, u:u + 255:2], ident[:])
+            nc.vector.tensor_copy(out=gb[:].rearrange("p (r u e) -> p u r e", u=2, e=2),
+                                  in_=gps[:, 0:256].bitcast(BF16).rearrange("p (u r e) -> p u r e", u=2, e=2)[:, :, 0:16, :])
+
+        h2 = const.tile([P, 4, 2048], F32, name="h2")
+        stats = const.tile([P, 4, 4, 6], F32, name="stats")
+        mv = const.tile([P, 4, 2], F32, name="mv")
+        veps = const.tile([P, 4], F32, name="veps")
+        rstd = const.tile([P, 4], F32, name="rstd")
+        ncod = [const.tile([P, 8 * 256], U32, name="ncod%d" % x, align_bytes=64) for x in range(2)]
+        nsca = [const.tile([P, 8 * 256], U8, name="nsca%d" % x, align_bytes=64) for x in range(2)]
+        acc1 = {}
+
+        def MM1(s, x):
+            hc, hs = codes[9 * x], scales[9 * x]
+            wc, ws = codes[s + 1], scales[s + 1]
+            acc = bank("acc1")
+            acc1[(s, x)] = acc
+            for b2 in range(2):
+                for g in range(4):
+                    lc = slice((b2 * 4 + g) * 128, (b2 * 4 + g + 1) * 128)
+                    rc = slice(g * 256, (g + 1) * 256)
+                    nc.tensor.matmul_mx(
+                        out=acc[:, b2 * 256:(b2 + 1) * 256],
+                        lhsT=hc[:, lc].bitcast(FP8X4), lhsT_scale=hs[:, lc],
+                        rhs=wc[:, rc].bitcast(FP8X4), rhs_scale=ws[:, rc],
+                        start=(g == 0), stop=(g == 3),
+                    )
+
+        def BIAS(s, x):
+            nc.vector.tensor_tensor(
+                out=h2[:, 2 * x:2 * x + 2, s * 256:(s + 1) * 256],
+                in0=acc1[(s, x)][:].rearrange("p (b n) -> p b n", b=2),
+                in1=bias1[:, s * 256:(s + 1) * 256].unsqueeze(1).to_broadcast([P, 2, 256]), op=ALU.add,
+            )
+
+        def TANH(s, x):
+            hv = h2[:, 2 * x:2 * x + 2, s * 256:(s + 1) * 256]
+            nc.scalar.activation(out=hv, in_=hv, func=ACT.Tanh)
+
+        def BN(bt, g):
+            nc.vector.bn_stats(out=stats[:, bt, g, :], in_=h2[:, bt, g * 512:(g + 1) * 512])
+
+        def STATS(x):
+            for bt in (2 * x, 2 * x + 1):
+                nc.vector.bn_aggr(out=mv[:, bt, :], in_=stats[:, bt, :, :].rearrange("p g s -> p (g s)"))
+            half = slice(2 * x, 2 * x + 2)
+            nc.vector.tensor_scalar(out=veps[:, half], in0=mv[:, half, 1], scalar1=LN_EPS, scalar2=None, op0=ALU.add)
+            nc.gpsimd.tensor_tensor(out=rstd[:, half], in0=veps[:, half], in1=mhalf[:, half], op=ALU.pow)
+
+        def Z(x, g):
+            for bt in (2 * x, 2 * x + 1):
+                hv = h2[:, bt, g * 512:(g + 1) * 512]
+                nc.vector.tensor_scalar(out=hv, in0=hv, scalar1=mv[:, bt, 0:1], scalar2=rstd[:, bt:bt + 1],
+                                        op0=ALU.subtract, op1=ALU.mult)
+
+        planes = {}
+        zts = {}
+        gns = {}
+
+        def ZT(x, g, u):
+            if u == 0:
+                for h in range(2):
+                    planes[(x, g, h)] = plp.tile([P, 4, 256], BF16, name="planes", tag="planes")
+            zt = bank("zt")
+            for e in range(2):
+                c0 = (2 * g + u) * 256 + e * 128
+                for b2 in range(2):
+                    j = 2 * e + b2
+                    nc.tensor.transpose(zt[:, j * 128:(j + 1) * 128], h2[:, 2 * x + b2, c0:c0 + 128], ident[:])
+            zts[(x, g, u)] = zt
+
+        def GB(x, g, u):
+            for h in range(2):
+                for e in range(2):
+                    t = 2 * u + e
+                    col = 16 * h + 4 * g + t
+                    nc.scalar.activation(out=planes[(x, g, h)][:, t, :], in_=zts[(x, g, u)][:, e * 256:(e + 1) * 256],
+                                         func=ACT.Identity, scale=gb[:, col:col + 1], bias=gb[:, 32 + col:33 + col])
+
+        def RG(x, g, h):
+            gn = gnp.tile([P, 256, 4], BF16, name="gn", tag="gn", align_bytes=64)
+            nc.vector.tensor_copy(
+                out=gn[:].rearrange("p (c i) t -> p c t i", i=4),
+                in_=planes[(x, g, h)][:].rearrange("p t (c i) -> p c t i", i=4),
+            )
+            gns[(x, g, h)] = gn
+
+        def QN(x, g, h):
+            kp = 4 * h + g
+            nc.vector.quantize_mx(out=ncod[x][:, kp * 256:(kp + 1) * 256].bitcast(FP8X4),
+                                  scales=nsca[x][:, kp * 256:(kp + 1) * 256],
+                                  in_=gns[(x, g, h)][:].rearrange("p b t -> p (b t)"))
+
+        acc2 = {}
+
+        def MM2(x, g, h):
+            kp = 4 * h + g
+            f = 10 + 2 * g + h
+            first = g == 0 and h == 0
+            last = g == 3 and h == 1
+            for b2 in range(2):
+                for cc in range(2):
+                    if first:
+                        acc2[(x, b2, cc)] = bank("acc2")
+                    lc = slice(kp * 256 + b2 * 128, kp * 256 + (b2 + 1) * 128)
+                    rc = slice(cc * 512, (cc + 1) * 512)
+                    nc.tensor.matmul_mx(
+                        out=acc2[(x, b2, cc)][:],
+                        lhsT=ncod[x][:, lc].bitcast(FP8X4), lhsT_scale=nsca[x][:, lc],
+                        rhs=codes[f][:, rc].bitcast(FP8X4), rhs_scale=scales[f][:, rc],
+                        start=first, stop=last,
+                    )
+                    if last:
+                        osb = osp.tile([P, 512], F32, name="osb", tag="osb")
+                        nc.vector.tensor_tensor(out=osb[:], in0=acc2[(x, b2, cc)][:], in1=fcb[:, rc], op=ALU.add)
+                        r0 = (2 * x + b2) * 128
+                        nc.sync.dma_start(out=out[r0:r0 + 128, rc], in_=osb[:])
+
+        def due(n, start, count):
+            d = n - start
+            if d >= 0 and d % 2 == 0 and d // 2 < count:
+                return d // 2
+            return None
+
+        T(0)
+        C(0, 0)
+        for c in range(4):
+            BM(c)
+        T(1)
+        C(1, 0)
+        Q(0)
+        BM(4)
+        BM(5)
+        GT()
+        T(2)
+        C(2, 0)
+        Q(1)
+        T(3)
+        for n in range(N_STEPS):
+            x, s = n // 8, n % 8
+            for xx in range(2):
+                for h in range(2):
+                    g = due(n, N0[xx] + RG_LAG[h] + 1, 4)
+                    if g is not None:
+                        QN(xx, g, h)
+            if n < 16:
+                MM1(s, x)
+            for xx in range(2):
+                for h in range(2):
+                    g = due(n, N0[xx] + MM_LAG[h], 4)
+                    if g is not None:
+                        MM2(xx, g, h)
+            T(n + 4)
+            for xx in range(2):
+                c = n - N0[xx]
+                if 0 <= c < 8:
+                    ZT(xx, c // 2, c % 2)
+            if 1 <= n <= 16:
+                TANH((n - 1) % 8, (n - 1) // 8)
+            C(n + 3, 1 if n >= 10 else 0)
+            for xx in range(2):
+                c = n - N0[xx] - 1
+                if 0 <= c < 8:
+                    GB(xx, c // 2, c % 2)
+            Q(n + 2)
+            if 2 <= n <= 16 and n % 2 == 0:
+                xx, g = (n - 1) // 8, ((n - 1) % 8) // 2
+                BN(2 * xx, g)
+                BN(2 * xx + 1, g)
+                if g == 3:
+                    STATS(xx)
+            for xx in range(2):
+                for h in range(2):
+                    g = due(n, N0[xx] + RG_LAG[h], 4)
+                    if g is not None:
+                        RG(xx, g, h)
+            if n < 16:
+                BIAS(s, x)
+            for xx in range(2):
+                g = due(n, N0[xx] - 1, 4)
+                if g is not None:
+                    Z(xx, g)

@@ -21,6 +21,15 @@ N0 = (10, 17)
 RG_LAG = (3, 4)
 MM_LAG = (4, 5)
 N_STEPS = 29
+LAST_BN = (9, 16)
+
+
+def n_sorted(pos):
+    return 2 if 4 <= pos <= 12 else 0
+
+
+def t_step(pos, half):
+    return pos - 4 if pos < 14 else 2 * pos - 18 + half
 
 
 def tile_rnnclassifier_pa_kernel(tc, h1, W_ih1, b_ih1, b_hh1, ln_g, ln_b, fc_W, fc_b, out):
@@ -28,6 +37,7 @@ def tile_rnnclassifier_pa_kernel(tc, h1, W_ih1, b_ih1, b_hh1, ln_g, ln_b, fc_W, 
     with ExitStack() as ctx:
         const = ctx.enter_context(tc.tile_pool(name="const", bufs=1))
         rawp = ctx.enter_context(tc.tile_pool(name="raw", bufs=4))
+        prmp = ctx.enter_context(tc.tile_pool(name="sorted", bufs=2))
         grpp = ctx.enter_context(tc.tile_pool(name="grouped", bufs=3))
         wfp = ctx.enter_context(tc.tile_pool(name="wfcodes", bufs=10))
         plp = ctx.enter_context(tc.tile_pool(name="planes", bufs=4))
@@ -39,18 +49,12 @@ def tile_rnnclassifier_pa_kernel(tc, h1, W_ih1, b_ih1, b_hh1, ln_g, ln_b, fc_W, 
         def bank(name):
             return psp.tile([P, 512], F32, name=name, tag="ps")
 
-        def slab_off(pos, i, a, u):
-            if pos == 0 or pos == 9:
-                return (i // 2) * 1024 + (2 * (i % 2) + a) * 256 + u
-            if pos < 9:
-                return a * 1024 + i * 256 + u
-            return (2 * i + a) * 256 + u
-
         raws = {}
         banks = {}
         groupeds = {}
         codes = {}
         scales = {}
+        perms = {}
         loaded = []
 
         def load():
@@ -69,6 +73,10 @@ def tile_rnnclassifier_pa_kernel(tc, h1, W_ih1, b_ih1, b_hh1, ln_g, ln_b, fc_W, 
             elif pos == 9:
                 nc.sync.dma_start(out=raw[:].rearrange("p (t k) -> p t k", t=2),
                                   in_=h1[256:512, :].rearrange("(t p) k -> p t k", p=P))
+            elif pos == 1:
+                for e in range(2):
+                    nc.sync.dma_start(out=raw[:, e * 2048:(e + 1) * 2048],
+                                      in_=W_ih1[0:512, :].rearrange("(q v e) k -> q v e k", v=2, e=2)[:, 0, e, :])
             elif pos < 9:
                 s = pos - 1
                 nc.sync.dma_start(out=raw[:], in_=W_ih1[(s // 2) * 512:(s // 2 + 1) * 512, :].rearrange("(q v e) k -> q v (e k)", v=2, e=2)[:, s % 2, :])
@@ -80,69 +88,91 @@ def tile_rnnclassifier_pa_kernel(tc, h1, W_ih1, b_ih1, b_hh1, ln_g, ln_b, fc_W, 
                     in_=fc_W[:, kp * 512:(kp + 1) * 512].rearrange("(c p) k -> p c k", p=P),
                 )
 
-        def T(pos):
-            if pos >= 18:
-                return
+        def T(pos, half):
             raw_w = raws[pos][:].bitcast(F32)
-            banks[pos] = []
-            for i in range(4):
+            banks.setdefault(pos, [])
+            for i in (2 * half, 2 * half + 1):
                 xt = bank("xt")
                 for a in range(2):
                     for u in range(2):
-                        o = slab_off(pos, i, a, u)
+                        o = (2 * i + a) * 256
                         j = 2 * a + u
-                        nc.tensor.transpose(xt[:, j * 128:(j + 1) * 128], raw_w[:, o:o + 255:2], ident[:])
+                        if i < n_sorted(pos):
+                            src = perms[pos][:, o + u * 128:o + (u + 1) * 128]
+                        else:
+                            src = raw_w[:, o + u:o + u + 255:2]
+                        nc.tensor.transpose(xt[:, j * 128:(j + 1) * 128], src, ident[:])
                 banks[pos].append(xt)
-            load()
+            if half == 1:
+                load()
 
-        def C(pos, vector_share):
-            if pos >= 18:
+        def S(pos):
+            if pos >= 18 or n_sorted(pos) == 0:
                 return
-            grouped = grpp.tile([P, 4096], BF16, name="grouped", tag="grouped", align_bytes=64)
-            gw = grouped[:].bitcast(F32)
-            for i in range(4):
-                dst = gw[:, i * 512:(i + 1) * 512].rearrange("p (a c u) -> p a c u", a=2, u=2)
+            nx = 2 * n_sorted(pos)
+            pw = prmp.tile([P, 2048], F32, name="pw", tag="pw")
+            perms[pos] = pw
+            nc.vector.tensor_copy(
+                out=pw[:, 0:nx * 256].rearrange("p (x u w) -> p x u w", x=nx, u=2),
+                in_=raws[pos][:].bitcast(F32)[:, 0:nx * 256].rearrange("p (x w u) -> p x u w", x=nx, u=2),
+            )
+
+        def C(pos, half, vector_share):
+            if half == 0:
+                groupeds[pos] = grpp.tile([P, 4096], BF16, name="grouped", tag="grouped", align_bytes=64)
+            gw = groupeds[pos][:].bitcast(F32)
+            for i in (2 * half, 2 * half + 1):
+                if 1 <= pos <= 8:
+                    e, j = i // 2, i % 2
+                    dst = gw.rearrange("p (j a e c u) -> p e j a c u", j=2, a=2, e=2, u=2)[:, e, j]
+                else:
+                    dst = gw[:, i * 512:(i + 1) * 512].rearrange("p (a c u) -> p a c u", a=2, u=2)
                 src = banks[pos][i][:].rearrange("p (a u c) -> p a c u", a=2, u=2)
-                if i >= 4 - vector_share:
+                if i % 2 >= 2 - vector_share:
                     nc.vector.tensor_copy(out=dst, in_=src)
                 else:
                     nc.scalar.copy(out=dst, in_=src)
-            groupeds[pos] = grouped
 
-        def Q(pos):
-            if pos >= 18:
-                return
-            if pos == 0 or pos == 9:
-                cd = const.tile([P, 1024], U32, name="hcd%d" % pos, align_bytes=64)
-                sc = const.tile([P, 1024], U8, name="hsc%d" % pos, align_bytes=64)
-            else:
-                cd = wfp.tile([P, 1024], U32, name="cd", tag="cd", align_bytes=64)
-                sc = wfp.tile([P, 1024], U8, name="sc", tag="sc", align_bytes=64)
-            nc.vector.quantize_mx(out=cd[:].bitcast(FP8X4), scales=sc[:], in_=groupeds[pos][:])
-            codes[pos] = cd
-            scales[pos] = sc
+        def Q(pos, part, parts):
+            if part == 0:
+                if pos == 0 or pos == 9:
+                    codes[pos] = const.tile([P, 1024], U32, name="hcd%d" % pos, align_bytes=64)
+                    scales[pos] = const.tile([P, 1024], U8, name="hsc%d" % pos, align_bytes=64)
+                else:
+                    codes[pos] = wfp.tile([P, 1024], U32, name="cd", tag="cd", align_bytes=64)
+                    scales[pos] = wfp.tile([P, 1024], U8, name="sc", tag="sc", align_bytes=64)
+            w = 1024 // parts
+            cols = slice(part * w, (part + 1) * w)
+            nc.vector.quantize_mx(out=codes[pos][:, cols].bitcast(FP8X4), scales=scales[pos][:, cols],
+                                  in_=groupeds[pos][:, part * 4 * w:(part + 1) * 4 * w])
 
-        for i in range(4):
-            load()
+        load()
 
         ident = const.tile([P, P], F32, name="ident")
         make_identity(nc, ident[:])
-        ones = const.tile([P, P], BF16, name="ones")
-        nc.vector.memset(ones[:], 1.0)
-        brow = const.tile([P, 3072], BF16, name="brow")
-        nc.vector.memset(brow[:], 0.0)
-        gl = const.tile([P, 512], BF16, name="gl")
-        nc.vector.memset(gl[:], 0.0)
-        mhalf = const.tile([P, 4], F32, name="mhalf")
-        nc.vector.memset(mhalf[:], -0.5)
         warm = const.tile([P, 1], F32, name="warm")
         nc.vector.memset(warm[:], 0.0)
-        nc.scalar.dma_start(out=brow[0:1, 0:2048], in_=b_ih1.rearrange("(o n) -> o n", o=1))
-        nc.scalar.dma_start(out=brow[1:2, 0:2048], in_=b_hh1.rearrange("(o n) -> o n", o=1))
-        nc.scalar.dma_start(out=brow[0:1, 2048:3072], in_=fc_b.rearrange("(o n) -> o n", o=1))
-        nc.scalar.dma_start(out=gl[0:8, :], in_=ln_g.rearrange("(r c) -> r c", c=512))
-        nc.scalar.dma_start(out=gl[8:16, :], in_=ln_b.rearrange("(r c) -> r c", c=512))
+        hid = const.tile([P, 512], BF16, name="hid")
+        nc.vector.memset(hid[:].bitcast(U32), 0)
+        cls = const.tile([P, 512], BF16, name="cls")
+        nc.vector.memset(cls[:].bitcast(U32), 0)
+        mhalf = const.tile([P, 4], F32, name="mhalf")
+        nc.vector.memset(mhalf[:], -0.5)
+
+        def load_rows(v, rows, r0):
+            nc.sync.dma_start(out=rows[r0:r0 + v.shape[0] // 512, :], in_=v.rearrange("(r c) -> r c", c=512))
+
+        load_rows(b_ih1, hid, 0)
+        load_rows(b_hh1, hid, 4)
+        for i in range(3):
+            load()
+        load_rows(fc_b, cls, 0)
+        load_rows(ln_g, cls, 2)
+        load_rows(ln_b, cls, 10)
         nc.scalar.activation(out=warm[:], in_=warm[:], func=ACT.Tanh)
+        sel = const.tile([P, 6], BF16, name="sel")
+        nc.vector.tensor_tensor(out=sel[:, 0:4], in0=ident[:, 0:4], in1=ident[:, 4:8], op=ALU.add)
+        nc.vector.tensor_copy(out=sel[:, 4:6], in_=ident[:, 0:2])
 
         bias1 = const.tile([P, 2048], F32, name="bias1")
         fcb = const.tile([P, 1024], F32, name="fcb")
@@ -150,7 +180,7 @@ def tile_rnnclassifier_pa_kernel(tc, h1, W_ih1, b_ih1, b_hh1, ln_g, ln_b, fc_W, 
 
         def BM(c):
             bp = bank("bp")
-            nc.tensor.matmul(out=bp[:], lhsT=ones[:], rhs=brow[:, c * 512:(c + 1) * 512], start=True, stop=True)
+            nc.tensor.matmul(out=bp[:], lhsT=sel[:, c:c + 1].to_broadcast([P, P]), rhs=(hid if c < 4 else cls)[:], start=True, stop=True)
             if c < 4:
                 nc.vector.tensor_copy(
                     out=bias1[:, c * 512:(c + 1) * 512].rearrange("p (t q) -> p t q", t=4),
@@ -162,9 +192,9 @@ def tile_rnnclassifier_pa_kernel(tc, h1, W_ih1, b_ih1, b_hh1, ln_g, ln_b, fc_W, 
         def GT():
             gps = bank("gps")
             for u in range(2):
-                nc.tensor.transpose(gps[:, u * 128:(u + 1) * 128], gl[:].bitcast(F32)[:, u:u + 255:2], ident[:])
+                nc.tensor.transpose(gps[:, u * 128:(u + 1) * 128], cls[:].bitcast(F32)[:, u:u + 255:2], ident[:])
             nc.vector.tensor_copy(out=gb[:].rearrange("p (r u e) -> p u r e", u=2, e=2),
-                                  in_=gps[:, 0:256].bitcast(BF16).rearrange("p (u r e) -> p u r e", u=2, e=2)[:, :, 0:16, :])
+                                  in_=gps[:, 0:256].bitcast(BF16).rearrange("p (u r e) -> p u r e", u=2, e=2)[:, :, 2:18, :])
 
         h2 = const.tile([P, 4, 2048], F32, name="h2")
         stats = const.tile([P, 4, 4, 6], F32, name="stats")
@@ -275,11 +305,15 @@ def tile_rnnclassifier_pa_kernel(tc, h1, W_ih1, b_ih1, b_hh1, ln_g, ln_b, fc_W, 
                         rhs=codes[f][:, rc].bitcast(FP8X4), rhs_scale=scales[f][:, rc],
                         start=first, stop=last,
                     )
-                    if last:
-                        osb = osp.tile([P, 512], F32, name="osb", tag="osb")
-                        nc.vector.tensor_tensor(out=osb[:], in0=acc2[(x, b2, cc)][:], in1=fcb[:, rc], op=ALU.add)
-                        r0 = (2 * x + b2) * 128
-                        nc.sync.dma_start(out=out[r0:r0 + 128, rc], in_=osb[:])
+
+        def OUT(x):
+            for b2 in range(2):
+                for cc in range(2):
+                    rc = slice(cc * 512, (cc + 1) * 512)
+                    osb = osp.tile([P, 512], F32, name="osb", tag="osb")
+                    nc.vector.tensor_tensor(out=osb[:], in0=acc2[(x, b2, cc)][:], in1=fcb[:, rc], op=ALU.add)
+                    r0 = (2 * x + b2) * 128
+                    nc.sync.dma_start(out=out[r0:r0 + 128, rc], in_=osb[:])
 
         def due(n, start, count):
             d = n - start
@@ -287,20 +321,21 @@ def tile_rnnclassifier_pa_kernel(tc, h1, W_ih1, b_ih1, b_hh1, ln_g, ln_b, fc_W, 
                 return d // 2
             return None
 
-        T(0)
-        C(0, 0)
-        for c in range(4):
-            BM(c)
-        T(1)
-        C(1, 0)
-        Q(0)
+        for pos in range(4):
+            for half in range(2):
+                T(pos, half)
+            if pos == 1:
+                for c in range(4):
+                    BM(c)
+            if pos < 3:
+                for half in range(2):
+                    C(pos, half, 1 if pos < 2 else half)
+            if 0 < pos < 3:
+                Q(pos - 1, 0, 1)
+        S(4)
         BM(4)
         BM(5)
         GT()
-        T(2)
-        C(2, 0)
-        Q(1)
-        T(3)
         for n in range(N_STEPS):
             x, s = n // 8, n % 8
             for xx in range(2):
@@ -308,6 +343,10 @@ def tile_rnnclassifier_pa_kernel(tc, h1, W_ih1, b_ih1, b_hh1, ln_g, ln_b, fc_W, 
                     g = due(n, N0[xx] + RG_LAG[h] + 1, 4)
                     if g is not None:
                         QN(xx, g, h)
+            for xx in range(2):
+                g = due(n, N0[xx], 4)
+                if g is not None:
+                    Z(xx, g)
             if n < 16:
                 MM1(s, x)
             for xx in range(2):
@@ -315,33 +354,52 @@ def tile_rnnclassifier_pa_kernel(tc, h1, W_ih1, b_ih1, b_hh1, ln_g, ln_b, fc_W, 
                     g = due(n, N0[xx] + MM_LAG[h], 4)
                     if g is not None:
                         MM2(xx, g, h)
-            T(n + 4)
+            for pos in range(4, 18):
+                for half in range(2):
+                    if t_step(pos, half) == n:
+                        T(pos, half)
             for xx in range(2):
                 c = n - N0[xx]
                 if 0 <= c < 8:
                     ZT(xx, c // 2, c % 2)
-            if 1 <= n <= 16:
+            if n == 16:
+                TANH(7, 1)
+            for pos in range(3, 18):
+                for half in range(2):
+                    if t_step(pos, half) == n - 1:
+                        C(pos, half, 0)
+            if 1 <= n <= 15:
                 TANH((n - 1) % 8, (n - 1) // 8)
-            C(n + 3, 1 if n >= 10 else 0)
             for xx in range(2):
                 c = n - N0[xx] - 1
                 if 0 <= c < 8:
                     GB(xx, c // 2, c % 2)
-            Q(n + 2)
-            if 2 <= n <= 16 and n % 2 == 0:
-                xx, g = (n - 1) // 8, ((n - 1) % 8) // 2
-                BN(2 * xx, g)
-                BN(2 * xx + 1, g)
-                if g == 3:
-                    STATS(xx)
             for xx in range(2):
                 for h in range(2):
                     g = due(n, N0[xx] + RG_LAG[h], 4)
                     if g is not None:
                         RG(xx, g, h)
+            for pos in range(2, 18):
+                if t_step(pos, 0) == t_step(pos, 1):
+                    if t_step(pos, 0) == n - 2:
+                        Q(pos, 0, 1)
+                else:
+                    for half in range(2):
+                        if t_step(pos, half) == n - 2:
+                            Q(pos, half, 2)
+            for xx in range(2):
+                d = n - 8 * xx - 3
+                if 0 <= d < 6:
+                    BN(2 * xx + d % 2, d // 2)
+                if n == LAST_BN[xx]:
+                    BN(2 * xx, 3)
+                    BN(2 * xx + 1, 3)
+                    STATS(xx)
+            for pos in range(5, 18):
+                if t_step(pos, 0) == n + 1:
+                    S(pos)
             if n < 16:
                 BIAS(s, x)
             for xx in range(2):
-                g = due(n, N0[xx] - 1, 4)
-                if g is not None:
-                    Z(xx, g)
+                if n == N0[xx] + MM_LAG[1] + 6:
+                    OUT(xx)

@@ -288,26 +288,26 @@ def tile_rnnclassifier_pa_kernel(tc, h1, W_ih1, b_ih1, b_hh1, ln_g, ln_b, fc_W, 
 
         acc2 = {}
 
-        def MM2(x, g, h):
-            kp = 4 * h + g
-            f = 10 + 2 * g + h
-            first = g == 0 and h == 0
-            last = g == 3 and h == 1
+        def MM2(x, g, hs):
             for b2 in range(2):
                 for cc in range(2):
-                    if first:
-                        acc2[(x, b2, cc)] = bank("acc2")
-                    lc = slice(kp * 256 + b2 * 128, kp * 256 + (b2 + 1) * 128)
-                    rc = slice(cc * 512, (cc + 1) * 512)
-                    nc.tensor.matmul_mx(
-                        out=acc2[(x, b2, cc)][:],
-                        lhsT=ncod[x][:, lc].bitcast(FP8X4), lhsT_scale=nsca[x][:, lc],
-                        rhs=codes[f][:, rc].bitcast(FP8X4), rhs_scale=scales[f][:, rc],
-                        start=first, stop=last,
-                    )
+                    for h in hs:
+                        kp = 4 * h + g
+                        f = 10 + 2 * g + h
+                        first = g == 0 and h == 0
+                        if first:
+                            acc2[(x, b2, cc)] = bank("acc2")
+                        lc = slice(kp * 256 + b2 * 128, kp * 256 + (b2 + 1) * 128)
+                        rc = slice(cc * 512, (cc + 1) * 512)
+                        nc.tensor.matmul_mx(
+                            out=acc2[(x, b2, cc)][:],
+                            lhsT=ncod[x][:, lc].bitcast(FP8X4), lhsT_scale=nsca[x][:, lc],
+                            rhs=codes[f][:, rc].bitcast(FP8X4), rhs_scale=scales[f][:, rc],
+                            start=first, stop=g == 3 and h == 1,
+                        )
 
-        def OUT(x):
-            for b2 in range(2):
+        def OUT(x, b2s):
+            for b2 in b2s:
                 for cc in range(2):
                     rc = slice(cc * 512, (cc + 1) * 512)
                     osb = osp.tile([P, 512], F32, name="osb", tag="osb")
@@ -349,19 +349,24 @@ def tile_rnnclassifier_pa_kernel(tc, h1, W_ih1, b_ih1, b_hh1, ln_g, ln_b, fc_W, 
                     Z(xx, g)
             if n < 16:
                 MM1(s, x)
-            for xx in range(2):
-                for h in range(2):
-                    g = due(n, N0[xx] + MM_LAG[h], 4)
-                    if g is not None:
-                        MM2(xx, g, h)
+            for h in range(2):
+                g = due(n, N0[0] + MM_LAG[h], 4)
+                if g is not None:
+                    MM2(0, g, (h,))
+            g = due(n, N0[1] + MM_LAG[1], 4)
+            if g is not None:
+                MM2(1, g, (0, 1))
             for pos in range(4, 18):
                 for half in range(2):
                     if t_step(pos, half) == n:
                         T(pos, half)
-            for xx in range(2):
-                c = n - N0[xx]
-                if 0 <= c < 8:
-                    ZT(xx, c // 2, c % 2)
+            c = n - N0[0]
+            if 0 <= c < 8:
+                ZT(0, c // 2, c % 2)
+            g = due(n, N0[1], 4)
+            if g is not None:
+                ZT(1, g, 0)
+                ZT(1, g, 1)
             if n == 16:
                 TANH(7, 1)
             for pos in range(3, 18):
@@ -400,6 +405,8 @@ def tile_rnnclassifier_pa_kernel(tc, h1, W_ih1, b_ih1, b_hh1, ln_g, ln_b, fc_W, 
                     S(pos)
             if n < 16:
                 BIAS(s, x)
-            for xx in range(2):
-                if n == N0[xx] + MM_LAG[1] + 6:
-                    OUT(xx)
+            d = n - N0[0] - MM_LAG[1] - 6
+            if 0 <= d < 2:
+                OUT(0, (d,))
+            if n == N0[1] + MM_LAG[1] + 6:
+                OUT(1, (0, 1))

@@ -25,7 +25,7 @@ LAST_BN = (9, 16)
 
 
 def n_sorted(pos):
-    return 2 if 4 <= pos <= 12 else 0
+    return 2 if 3 <= pos <= 12 else 0
 
 
 def t_step(pos, half):
@@ -97,7 +97,7 @@ def tile_rnnclassifier_pa_kernel(tc, h1, W_ih1, b_ih1, b_hh1, ln_g, ln_b, fc_W, 
                     for u in range(2):
                         o = (2 * i + a) * 256
                         j = 2 * a + u
-                        if i < n_sorted(pos):
+                        if i >= 4 - n_sorted(pos):
                             src = perms[pos][:, o + u * 128:o + (u + 1) * 128]
                         else:
                             src = raw_w[:, o + u:o + u + 255:2]
@@ -110,11 +110,12 @@ def tile_rnnclassifier_pa_kernel(tc, h1, W_ih1, b_ih1, b_hh1, ln_g, ln_b, fc_W, 
             if pos >= 18 or n_sorted(pos) == 0:
                 return
             nx = 2 * n_sorted(pos)
+            w0 = 2048 - nx * 256
             pw = prmp.tile([P, 2048], F32, name="pw", tag="pw")
             perms[pos] = pw
             nc.vector.tensor_copy(
-                out=pw[:, 0:nx * 256].rearrange("p (x u w) -> p x u w", x=nx, u=2),
-                in_=raws[pos][:].bitcast(F32)[:, 0:nx * 256].rearrange("p (x w u) -> p x u w", x=nx, u=2),
+                out=pw[:, w0:2048].rearrange("p (x u w) -> p x u w", x=nx, u=2),
+                in_=raws[pos][:].bitcast(F32)[:, w0:2048].rearrange("p (x w u) -> p x u w", x=nx, u=2),
             )
 
         def C(pos, half, vector_share):
@@ -164,11 +165,12 @@ def tile_rnnclassifier_pa_kernel(tc, h1, W_ih1, b_ih1, b_hh1, ln_g, ln_b, fc_W, 
 
         load_rows(b_ih1, hid, 0)
         load_rows(b_hh1, hid, 4)
-        for i in range(3):
-            load()
+        load()
         load_rows(fc_b, cls, 0)
         load_rows(ln_g, cls, 2)
         load_rows(ln_b, cls, 10)
+        for i in range(2):
+            load()
         nc.scalar.activation(out=warm[:], in_=warm[:], func=ACT.Tanh)
         sel = const.tile([P, 6], BF16, name="sel")
         nc.vector.tensor_tensor(out=sel[:, 0:4], in0=ident[:, 0:4], in1=ident[:, 4:8], op=ALU.add)
@@ -182,7 +184,7 @@ def tile_rnnclassifier_pa_kernel(tc, h1, W_ih1, b_ih1, b_hh1, ln_g, ln_b, fc_W, 
             bp = bank("bp")
             nc.tensor.matmul(out=bp[:], lhsT=sel[:, c:c + 1].to_broadcast([P, P]), rhs=(hid if c < 4 else cls)[:], start=True, stop=True)
             if c < 4:
-                nc.vector.tensor_copy(
+                nc.scalar.copy(
                     out=bias1[:, c * 512:(c + 1) * 512].rearrange("p (t q) -> p t q", t=4),
                     in_=bp[:].rearrange("p (q t) -> p t q", t=4),
                 )
@@ -197,7 +199,7 @@ def tile_rnnclassifier_pa_kernel(tc, h1, W_ih1, b_ih1, b_hh1, ln_g, ln_b, fc_W, 
                                   in_=gps[:, 0:256].bitcast(BF16).rearrange("p (u r e) -> p u r e", u=2, e=2)[:, :, 2:18, :])
 
         h2 = const.tile([P, 4, 2048], F32, name="h2")
-        stats = const.tile([P, 4, 4, 6], F32, name="stats")
+        stats = const.tile([P, 2, 8, 6], F32, name="stats")
         mv = const.tile([P, 4, 2], F32, name="mv")
         veps = const.tile([P, 4], F32, name="veps")
         rstd = const.tile([P, 4], F32, name="rstd")
@@ -232,12 +234,13 @@ def tile_rnnclassifier_pa_kernel(tc, h1, W_ih1, b_ih1, b_hh1, ln_g, ln_b, fc_W, 
             hv = h2[:, 2 * x:2 * x + 2, s * 256:(s + 1) * 256]
             nc.scalar.activation(out=hv, in_=hv, func=ACT.Tanh)
 
-        def BN(bt, g):
-            nc.vector.bn_stats(out=stats[:, bt, g, :], in_=h2[:, bt, g * 512:(g + 1) * 512])
+        def BN(s, x):
+            nc.vector.bn_stats(out=stats[:, x, s, :],
+                               in_=h2[:, 2 * x:2 * x + 2, s * 256:(s + 1) * 256].rearrange("p b n -> p n b"))
 
         def STATS(x):
-            for bt in (2 * x, 2 * x + 1):
-                nc.vector.bn_aggr(out=mv[:, bt, :], in_=stats[:, bt, :, :].rearrange("p g s -> p (g s)"))
+            for b2 in range(2):
+                nc.vector.bn_aggr(out=mv[:, 2 * x + b2, :], in_=stats[:, x, :, 3 * b2:3 * b2 + 3])
             half = slice(2 * x, 2 * x + 2)
             nc.vector.tensor_scalar(out=veps[:, half], in0=mv[:, half, 1], scalar1=LN_EPS, scalar2=None, op0=ALU.add)
             nc.gpsimd.tensor_tensor(out=rstd[:, half], in0=veps[:, half], in1=mhalf[:, half], op=ALU.pow)
@@ -324,18 +327,17 @@ def tile_rnnclassifier_pa_kernel(tc, h1, W_ih1, b_ih1, b_hh1, ln_g, ln_b, fc_W, 
         for pos in range(4):
             for half in range(2):
                 T(pos, half)
-            if pos == 1:
-                for c in range(4):
-                    BM(c)
             if pos < 3:
                 for half in range(2):
-                    C(pos, half, 1 if pos < 2 else half)
-            if 0 < pos < 3:
-                Q(pos - 1, 0, 1)
-        S(4)
-        BM(4)
-        BM(5)
-        GT()
+                    C(pos, half, 1 if pos == 0 else 0)
+            if pos == 1:
+                for c in range(6):
+                    BM(c)
+                GT()
+            if pos < 2:
+                Q(pos, 0, 1)
+            if pos in (1, 2):
+                S(pos + 2)
         for n in range(N_STEPS):
             x, s = n // 8, n % 8
             for xx in range(2):
@@ -384,6 +386,12 @@ def tile_rnnclassifier_pa_kernel(tc, h1, W_ih1, b_ih1, b_hh1, ln_g, ln_b, fc_W, 
                     g = due(n, N0[xx] + RG_LAG[h], 4)
                     if g is not None:
                         RG(xx, g, h)
+            for xx in range(2):
+                for sl in range(8):
+                    if n == min(8 * xx + sl + 2, 16):
+                        BN(sl, xx)
+                if n == LAST_BN[xx]:
+                    STATS(xx)
             for pos in range(2, 18):
                 if t_step(pos, 0) == t_step(pos, 1):
                     if t_step(pos, 0) == n - 2:
@@ -392,21 +400,13 @@ def tile_rnnclassifier_pa_kernel(tc, h1, W_ih1, b_ih1, b_hh1, ln_g, ln_b, fc_W, 
                     for half in range(2):
                         if t_step(pos, half) == n - 2:
                             Q(pos, half, 2)
-            for xx in range(2):
-                d = n - 8 * xx - 3
-                if 0 <= d < 6:
-                    BN(2 * xx + d % 2, d // 2)
-                if n == LAST_BN[xx]:
-                    BN(2 * xx, 3)
-                    BN(2 * xx + 1, 3)
-                    STATS(xx)
             for pos in range(5, 18):
                 if t_step(pos, 0) == n + 1:
                     S(pos)
             if n < 16:
                 BIAS(s, x)
-            d = n - N0[0] - MM_LAG[1] - 6
-            if 0 <= d < 2:
-                OUT(0, (d,))
+            if n == N0[0] + MM_LAG[1] + 6:
+                OUT(0, (0,))
             if n == N0[1] + MM_LAG[1] + 6:
+                OUT(0, (1,))
                 OUT(1, (0, 1))

@@ -42,7 +42,7 @@ def tile_rnnclassifier_pa_kernel(tc, h1, W_ih1, b_ih1, b_hh1, ln_g, ln_b, fc_W, 
         wfp = ctx.enter_context(tc.tile_pool(name="wfcodes", bufs=10))
         plp = ctx.enter_context(tc.tile_pool(name="planes", bufs=4))
         gnp = ctx.enter_context(tc.tile_pool(name="gnorm", bufs=3))
-        osp = ctx.enter_context(tc.tile_pool(name="outs", bufs=4))
+        osp = ctx.enter_context(tc.tile_pool(name="outs", bufs=8))
         psp = ctx.enter_context(tc.psum_pool(name="psum", bufs=8))
         ctx.enter_context(tc.manual_schedule())
 
@@ -104,6 +104,8 @@ def tile_rnnclassifier_pa_kernel(tc, h1, W_ih1, b_ih1, b_hh1, ln_g, ln_b, fc_W, 
                         nc.tensor.transpose(xt[:, j * 128:(j + 1) * 128], src, ident[:])
                 banks[pos].append(xt)
             if half == 1:
+                if len(loaded) == 18 and pos == 14:
+                    nc.sync.dma_start(out=fcb[:], in_=fc_b.partition_broadcast(P))
                 load()
 
         def S(pos):
@@ -166,37 +168,32 @@ def tile_rnnclassifier_pa_kernel(tc, h1, W_ih1, b_ih1, b_hh1, ln_g, ln_b, fc_W, 
         load_rows(b_ih1, hid, 0)
         load_rows(b_hh1, hid, 4)
         load()
-        load_rows(fc_b, cls, 0)
-        load_rows(ln_g, cls, 2)
-        load_rows(ln_b, cls, 10)
+        load_rows(ln_g, cls, 0)
+        load_rows(ln_b, cls, 8)
         for i in range(2):
             load()
         nc.scalar.activation(out=warm[:], in_=warm[:], func=ACT.Tanh)
-        sel = const.tile([P, 6], BF16, name="sel")
-        nc.vector.tensor_tensor(out=sel[:, 0:4], in0=ident[:, 0:4], in1=ident[:, 4:8], op=ALU.add)
-        nc.vector.tensor_copy(out=sel[:, 4:6], in_=ident[:, 0:2])
+        sel = const.tile([P, 4], BF16, name="sel")
+        nc.vector.tensor_tensor(out=sel[:], in0=ident[:, 0:4], in1=ident[:, 4:8], op=ALU.add)
 
         bias1 = const.tile([P, 2048], F32, name="bias1")
-        fcb = const.tile([P, 1024], F32, name="fcb")
+        fcb = const.tile([P, 1024], BF16, name="fcb")
         gb = const.tile([P, 64], F32, name="gb")
 
         def BM(c):
             bp = bank("bp")
-            nc.tensor.matmul(out=bp[:], lhsT=sel[:, c:c + 1].to_broadcast([P, P]), rhs=(hid if c < 4 else cls)[:], start=True, stop=True)
-            if c < 4:
-                nc.scalar.copy(
-                    out=bias1[:, c * 512:(c + 1) * 512].rearrange("p (t q) -> p t q", t=4),
-                    in_=bp[:].rearrange("p (q t) -> p t q", t=4),
-                )
-            else:
-                nc.vector.tensor_copy(out=fcb[:, (c - 4) * 512:(c - 3) * 512], in_=bp[:])
+            nc.tensor.matmul(out=bp[:], lhsT=sel[:, c:c + 1].to_broadcast([P, P]), rhs=hid[:], start=True, stop=True)
+            nc.scalar.copy(
+                out=bias1[:, c * 512:(c + 1) * 512].rearrange("p (t q) -> p t q", t=4),
+                in_=bp[:].rearrange("p (q t) -> p t q", t=4),
+            )
 
         def GT():
             gps = bank("gps")
             for u in range(2):
                 nc.tensor.transpose(gps[:, u * 128:(u + 1) * 128], cls[:].bitcast(F32)[:, u:u + 255:2], ident[:])
             nc.vector.tensor_copy(out=gb[:].rearrange("p (r u e) -> p u r e", u=2, e=2),
-                                  in_=gps[:, 0:256].bitcast(BF16).rearrange("p (u r e) -> p u r e", u=2, e=2)[:, :, 2:18, :])
+                                  in_=gps[:, 0:256].bitcast(BF16).rearrange("p (u r e) -> p u r e", u=2, e=2)[:, :, 0:16, :])
 
         h2 = const.tile([P, 4, 2048], F32, name="h2")
         stats = const.tile([P, 2, 8, 6], F32, name="stats")
@@ -331,7 +328,7 @@ def tile_rnnclassifier_pa_kernel(tc, h1, W_ih1, b_ih1, b_hh1, ln_g, ln_b, fc_W, 
                 for half in range(2):
                     C(pos, half, 1 if pos == 0 else 0)
             if pos == 1:
-                for c in range(6):
+                for c in range(4):
                     BM(c)
                 GT()
             if pos < 2:

@@ -274,10 +274,12 @@ def tile_rnnclassifier_pa_kernel(tc, h1, W_ih1, b_ih1, b_hh1, ln_g, ln_b, fc_W, 
 
         def RG(x, g, h):
             gn = gnp.tile([P, 256, 4], BF16, name="gn", tag="gn", align_bytes=64)
-            nc.vector.tensor_copy(
-                out=gn[:].rearrange("p (c i) t -> p c t i", i=4),
-                in_=planes[(x, g, h)][:].rearrange("p t (c i) -> p c t i", i=4),
-            )
+            dst = gn[:].rearrange("p (c i) t -> p c t i", i=4)
+            src = planes[(x, g, h)][:].rearrange("p t (c i) -> p c t i", i=4)
+            if (x, g, h) == (1, 3, 1):
+                nc.scalar.copy(out=dst, in_=src)
+            else:
+                nc.vector.tensor_copy(out=dst, in_=src)
             gns[(x, g, h)] = gn
 
         def QN(x, g, h):
@@ -309,11 +311,14 @@ def tile_rnnclassifier_pa_kernel(tc, h1, W_ih1, b_ih1, b_hh1, ln_g, ln_b, fc_W, 
         def OUT(x, b2s):
             for b2 in b2s:
                 for cc in range(2):
-                    rc = slice(cc * 512, (cc + 1) * 512)
                     osb = osp.tile([P, 512], F32, name="osb", tag="osb")
-                    nc.vector.tensor_tensor(out=osb[:], in0=acc2[(x, b2, cc)][:], in1=fcb[:, rc], op=ALU.add)
                     r0 = (2 * x + b2) * 128
-                    nc.sync.dma_start(out=out[r0:r0 + 128, rc], in_=osb[:])
+                    w = 256 if (x, b2, cc) == (1, 1, 1) else 512
+                    for c0 in range(0, 512, w):
+                        c1 = cc * 512 + c0
+                        nc.vector.tensor_tensor(out=osb[:, c0:c0 + w], in0=acc2[(x, b2, cc)][:, c0:c0 + w],
+                                                in1=fcb[:, c1:c1 + w], op=ALU.add)
+                        nc.sync.dma_start(out=out[r0:r0 + 128, c1:c1 + w], in_=osb[:, c0:c0 + w])
 
         def due(n, start, count):
             d = n - start

@@ -122,7 +122,7 @@ def tile_rnnclassifier_pa_kernel(tc, h1, W_ih1, b_ih1, b_hh1, ln_g, ln_b, fc_W, 
 
         def C(pos, half, vector_share):
             if half == 0:
-                groupeds[pos] = grpp.tile([P, 4096], BF16, name="grouped", tag="grouped", align_bytes=64)
+                groupeds[pos] = grpp.tile([P, 4096], BF16, name="grouped", tag="grouped", align_bytes=256)
             gw = groupeds[pos][:].bitcast(F32)
             for i in (2 * half, 2 * half + 1):
                 if 1 <= pos <= 8:
@@ -139,11 +139,11 @@ def tile_rnnclassifier_pa_kernel(tc, h1, W_ih1, b_ih1, b_hh1, ln_g, ln_b, fc_W, 
         def Q(pos, part, parts):
             if part == 0:
                 if pos == 0 or pos == 9:
-                    codes[pos] = const.tile([P, 1024], U32, name="hcd%d" % pos, align_bytes=64)
-                    scales[pos] = const.tile([P, 1024], U8, name="hsc%d" % pos, align_bytes=64)
+                    codes[pos] = const.tile([P, 1024], U32, name="hcd%d" % pos, align_bytes=256)
+                    scales[pos] = const.tile([P, 1024], U8, name="hsc%d" % pos, align_bytes=256)
                 else:
-                    codes[pos] = wfp.tile([P, 1024], U32, name="cd", tag="cd", align_bytes=64)
-                    scales[pos] = wfp.tile([P, 1024], U8, name="sc", tag="sc", align_bytes=64)
+                    codes[pos] = wfp.tile([P, 1024], U32, name="cd", tag="cd", align_bytes=256)
+                    scales[pos] = wfp.tile([P, 1024], U8, name="sc", tag="sc", align_bytes=256)
             w = 1024 // parts
             cols = slice(part * w, (part + 1) * w)
             nc.vector.quantize_mx(out=codes[pos][:, cols].bitcast(FP8X4), scales=scales[pos][:, cols],
@@ -200,8 +200,8 @@ def tile_rnnclassifier_pa_kernel(tc, h1, W_ih1, b_ih1, b_hh1, ln_g, ln_b, fc_W, 
         mv = const.tile([P, 4, 2], F32, name="mv")
         veps = const.tile([P, 4], F32, name="veps")
         rstd = const.tile([P, 4], F32, name="rstd")
-        ncod = [const.tile([P, 8 * 256], U32, name="ncod%d" % x, align_bytes=64) for x in range(2)]
-        nsca = [const.tile([P, 8 * 256], U8, name="nsca%d" % x, align_bytes=64) for x in range(2)]
+        ncod = [const.tile([P, 8 * 256], U32, name="ncod%d" % x, align_bytes=256) for x in range(2)]
+        nsca = [const.tile([P, 8 * 256], U8, name="nsca%d" % x, align_bytes=256) for x in range(2)]
         acc1 = {}
 
         def MM1(s, x):
@@ -273,7 +273,7 @@ def tile_rnnclassifier_pa_kernel(tc, h1, W_ih1, b_ih1, b_hh1, ln_g, ln_b, fc_W, 
                                          func=ACT.Identity, scale=gb[:, col:col + 1], bias=gb[:, 32 + col:33 + col])
 
         def RG(x, g, h):
-            gn = gnp.tile([P, 256, 4], BF16, name="gn", tag="gn", align_bytes=64)
+            gn = gnp.tile([P, 256, 4], BF16, name="gn", tag="gn", align_bytes=256)
             dst = gn[:].rearrange("p (c i) t -> p c t i", i=4)
             src = planes[(x, g, h)][:].rearrange("p t (c i) -> p c t i", i=4)
             if (x, g, h) == (1, 3, 1):

from contextlib import ExitStack

import concourse.mybir as mybir
from concourse.masks import make_identity

F32 = mybir.dt.float32
BF16 = mybir.dt.bfloat16
U32 = mybir.dt.uint32
U8 = mybir.dt.uint8
FP8X4 = mybir.dt.float8_e4m3fn_x4
ALU = mybir.AluOpType
ACT = mybir.ActivationFunctionType

P = 128
B, H, D_OUT = 512, 2048, 1024
LN_EPS = 1e-5
FLOPS = 2 * B * H * H + 2 * B * 2 * H * D_OUT


N0 = (10, 17)
RG_LAG = (3, 4)
MM_LAG = (4, 5)
N_STEPS = 29
LAST_BN = (9, 16)


def n_sorted(pos):
    return 2 if 3 <= pos <= 12 else 0


def t_step(pos, half):
    return pos - 4 if pos < 14 else 2 * pos - 18 + half


def tile_rnnclassifier_pa_kernel(tc, h1, W_ih1, b_ih1, b_hh1, ln_g, ln_b, fc_W, fc_b, out):
    nc = tc.nc
    with ExitStack() as ctx:
        const = ctx.enter_context(tc.tile_pool(name="const", bufs=1))
        rawp = ctx.enter_context(tc.tile_pool(name="raw", bufs=4))
        prmp = ctx.enter_context(tc.tile_pool(name="sorted", bufs=2))
        grpp = ctx.enter_context(tc.tile_pool(name="grouped", bufs=3))
        wfp = ctx.enter_context(tc.tile_pool(name="wfcodes", bufs=10))
        plp = ctx.enter_context(tc.tile_pool(name="planes", bufs=4))
        gnp = ctx.enter_context(tc.tile_pool(name="gnorm", bufs=3))
        osp = ctx.enter_context(tc.tile_pool(name="outs", bufs=8))
        psp = ctx.enter_context(tc.psum_pool(name="psum", bufs=8))
        ctx.enter_context(tc.manual_schedule())

        def bank(name):
            return psp.tile([P, 512], F32, name=name, tag="ps")

        raws = {}
        banks = {}
        groupeds = {}
        codes = {}
        scales = {}
        perms = {}
        loaded = []

        def load():
            pos = len(loaded)
            if pos >= 18:
                return
            loaded.append(pos)
            raw = rawp.tile([P, 4096], BF16, name="raw", tag="raw")
            raws[pos] = raw
            if pos == 0:
                for i in range(4):
                    nc.sync.dma_start(
                        out=raw[:, i * 1024:(i + 1) * 1024],
                        in_=h1[(i // 2) * 128:(i // 2 + 1) * 128, (i % 2) * 1024:(i % 2 + 1) * 1024],
                    )
            elif pos == 9:
                nc.sync.dma_start(out=raw[:].rearrange("p (t k) -> p t k", t=2),
                                  in_=h1[256:512, :].rearrange("(t p) k -> p t k", p=P))
            elif pos == 1:
                for e in range(2):
                    nc.sync.dma_start(out=raw[:, e * 2048:(e + 1) * 2048],
                                      in_=W_ih1[0:512, :].rearrange("(q v e) k -> q v e k", v=2, e=2)[:, 0, e, :])
            elif pos < 9:
                s = pos - 1
                nc.sync.dma_start(out=raw[:], in_=W_ih1[(s // 2) * 512:(s // 2 + 1) * 512, :].rearrange("(q v e) k -> q v (e k)", v=2, e=2)[:, s % 2, :])
            else:
                f = pos - 10
                kp = 4 * (f % 2) + f // 2
                nc.sync.dma_start(
                    out=raw[:].rearrange("p (c k) -> p c k", c=8),
                    in_=fc_W[:, kp * 512:(kp + 1) * 512].rearrange("(c p) k -> p c k", p=P),
                )

        def T(pos, half):
            raw_w = raws[pos][:].bitcast(F32)
            banks.setdefault(pos, [])
            for i in (2 * half, 2 * half + 1):
                xt = bank("xt")
                for a in range(2):
                    for u in range(2):
                        o = (2 * i + a) * 256
                        j = 2 * a + u
                        if i >= 4 - n_sorted(pos):
                            src = perms[pos][:, o + u * 128:o + (u + 1) * 128]
                        else:
                            src = raw_w[:, o + u:o + u + 255:2]
                        nc.tensor.transpose(xt[:, j * 128:(j + 1) * 128], src, ident[:])
                banks[pos].append(xt)
            if half == 1:
                if len(loaded) == 18 and pos == 14:
                    nc.sync.dma_start(out=fcb[:], in_=fc_b.partition_broadcast(P))
                load()

        def S(pos):
            if pos >= 18 or n_sorted(pos) == 0:
                return
            nx = 2 * n_sorted(pos)
            w0 = 2048 - nx * 256
            pw = prmp.tile([P, 2048], F32, name="pw", tag="pw")
            perms[pos] = pw
            nc.vector.tensor_copy(
                out=pw[:, w0:2048].rearrange("p (x u w) -> p x u w", x=nx, u=2),
                in_=raws[pos][:].bitcast(F32)[:, w0:2048].rearrange("p (x w u) -> p x u w", x=nx, u=2),
            )

        def C(pos, half, vector_share):
            if half == 0:
                groupeds[pos] = grpp.tile([P, 4096], BF16, name="grouped", tag="grouped", align_bytes=256)
            gw = groupeds[pos][:].bitcast(F32)
            for i in (2 * half, 2 * half + 1):
                if 1 <= pos <= 8:
                    e, j = i // 2, i % 2
                    dst = gw.rearrange("p (j a e c u) -> p e j a c u", j=2, a=2, e=2, u=2)[:, e, j]
                else:
                    dst = gw[:, i * 512:(i + 1) * 512].rearrange("p (a c u) -> p a c u", a=2, u=2)
                src = banks[pos][i][:].rearrange("p (a u c) -> p a c u", a=2, u=2)
                if i % 2 >= 2 - vector_share:
                    nc.vector.tensor_copy(out=dst, in_=src)
                else:
                    nc.scalar.copy(out=dst, in_=src)

        def Q(pos, part, parts):
            if part == 0:
                if pos == 0 or pos == 9:
                    codes[pos] = const.tile([P, 1024], U32, name="hcd%d" % pos, align_bytes=256)
                    scales[pos] = const.tile([P, 1024], U8, name="hsc%d" % pos, align_bytes=256)
                else:
                    codes[pos] = wfp.tile([P, 1024], U32, name="cd", tag="cd", align_bytes=256)
                    scales[pos] = wfp.tile([P, 1024], U8, name="sc", tag="sc", align_bytes=256)
            w = 1024 // parts
            cols = slice(part * w, (part + 1) * w)
            nc.vector.quantize_mx(out=codes[pos][:, cols].bitcast(FP8X4), scales=scales[pos][:, cols],
                                  in_=groupeds[pos][:, part * 4 * w:(part + 1) * 4 * w])

        load()

        ident = const.tile([P, P], F32, name="ident")
        make_identity(nc, ident[:])
        warm = const.tile([P, 1], F32, name="warm")
        nc.vector.memset(warm[:], 0.0)
        hid = const.tile([P, 512], BF16, name="hid")
        nc.vector.memset(hid[:].bitcast(U32), 0)
        cls = const.tile([P, 512], BF16, name="cls")
        nc.vector.memset(cls[:].bitcast(U32), 0)
        mhalf = const.tile([P, 4], F32, name="mhalf")
        nc.vector.memset(mhalf[:], -0.5)

        def load_rows(v, rows, r0):
            nc.sync.dma_start(out=rows[r0:r0 + v.shape[0] // 512, :], in_=v.rearrange("(r c) -> r c", c=512))

        load_rows(b_ih1, hid, 0)
        load_rows(b_hh1, hid, 4)
        load()
        load_rows(ln_g, cls, 0)
        load_rows(ln_b, cls, 8)
        for i in range(2):
            load()
        nc.scalar.activation(out=warm[:], in_=warm[:], func=ACT.Tanh)
        sel = const.tile([P, 4], BF16, name="sel")
        nc.vector.tensor_tensor(out=sel[:], in0=ident[:, 0:4], in1=ident[:, 4:8], op=ALU.add)

        bias1 = const.tile([P, 2048], F32, name="bias1")
        fcb = const.tile([P, 1024], BF16, name="fcb")
        gb = const.tile([P, 64], F32, name="gb")

        def BM(c):
            bp = bank("bp")
            nc.tensor.matmul(out=bp[:], lhsT=sel[:, c:c + 1].to_broadcast([P, P]), rhs=hid[:], start=True, stop=True)
            nc.scalar.copy(
                out=bias1[:, c * 512:(c + 1) * 512].rearrange("p (t q) -> p t q", t=4),
                in_=bp[:].rearrange("p (q t) -> p t q", t=4),
            )

        def GT():
            gps = bank("gps")
            for u in range(2):
                nc.tensor.transpose(gps[:, u * 128:(u + 1) * 128], cls[:].bitcast(F32)[:, u:u + 255:2], ident[:])
            nc.vector.tensor_copy(out=gb[:].rearrange("p (r u e) -> p u r e", u=2, e=2),
                                  in_=gps[:, 0:256].bitcast(BF16).rearrange("p (u r e) -> p u r e", u=2, e=2)[:, :, 0:16, :])

        h2 = const.tile([P, 4, 2048], F32, name="h2")
        stats = const.tile([P, 2, 8, 6], F32, name="stats")
        mv = const.tile([P, 4, 2], F32, name="mv")
        veps = const.tile([P, 4], F32, name="veps")
        rstd = const.tile([P, 4], F32, name="rstd")
        ncod = [const.tile([P, 8 * 256], U32, name="ncod%d" % x, align_bytes=256) for x in range(2)]
        nsca = [const.tile([P, 8 * 256], U8, name="nsca%d" % x, align_bytes=256) for x in range(2)]
        acc1 = {}

        def MM1(s, x):
            hc, hs = codes[9 * x], scales[9 * x]
            wc, ws = codes[s + 1], scales[s + 1]
            acc = bank("acc1")
            acc1[(s, x)] = acc
            for b2 in range(2):
                for g in range(4):
                    lc = slice((b2 * 4 + g) * 128, (b2 * 4 + g + 1) * 128)
                    rc = slice(g * 256, (g + 1) * 256)
                    nc.tensor.matmul_mx(
                        out=acc[:, b2 * 256:(b2 + 1) * 256],
                        lhsT=hc[:, lc].bitcast(FP8X4), lhsT_scale=hs[:, lc],
                        rhs=wc[:, rc].bitcast(FP8X4), rhs_scale=ws[:, rc],
                        start=(g == 0), stop=(g == 3),
                    )

        def BIAS(s, x):
            nc.vector.tensor_tensor(
                out=h2[:, 2 * x:2 * x + 2, s * 256:(s + 1) * 256],
                in0=acc1[(s, x)][:].rearrange("p (b n) -> p b n", b=2),
                in1=bias1[:, s * 256:(s + 1) * 256].unsqueeze(1).to_broadcast([P, 2, 256]), op=ALU.add,
            )

        def TANH(s, x):
            hv = h2[:, 2 * x:2 * x + 2, s * 256:(s + 1) * 256]
            nc.scalar.activation(out=hv, in_=hv, func=ACT.Tanh)

        def BN(s, x):
            nc.vector.bn_stats(out=stats[:, x, s, :],
                               in_=h2[:, 2 * x:2 * x + 2, s * 256:(s + 1) * 256].rearrange("p b n -> p n b"))

        def STATS(x):
            for b2 in range(2):
                nc.vector.bn_aggr(out=mv[:, 2 * x + b2, :], in_=stats[:, x, :, 3 * b2:3 * b2 + 3])
            half = slice(2 * x, 2 * x + 2)
            nc.vector.tensor_scalar(out=veps[:, half], in0=mv[:, half, 1], scalar1=LN_EPS, scalar2=None, op0=ALU.add)
            nc.gpsimd.tensor_tensor(out=rstd[:, half], in0=veps[:, half], in1=mhalf[:, half], op=ALU.pow)

        def Z(x, g):
            for bt in (2 * x, 2 * x + 1):
                hv = h2[:, bt, g * 512:(g + 1) * 512]
                nc.vector.tensor_scalar(out=hv, in0=hv, scalar1=mv[:, bt, 0:1], scalar2=rstd[:, bt:bt + 1],
                                        op0=ALU.subtract, op1=ALU.mult)

        planes = {}
        zts = {}
        gns = {}

        def ZT(x, g, u):
            if u == 0:
                for h in range(2):
                    planes[(x, g, h)] = plp.tile([P, 4, 256], BF16, name="planes", tag="planes")
            zt = bank("zt")
            for e in range(2):
                c0 = (2 * g + u) * 256 + e * 128
                for b2 in range(2):
                    j = 2 * e + b2
                    nc.tensor.transpose(zt[:, j * 128:(j + 1) * 128], h2[:, 2 * x + b2, c0:c0 + 128], ident[:])
            zts[(x, g, u)] = zt

        def GB(x, g, u):
            for h in range(2):
                for e in range(2):
                    t = 2 * u + e
                    col = 16 * h + 4 * g + t
                    nc.scalar.activation(out=planes[(x, g, h)][:, t, :], in_=zts[(x, g, u)][:, e * 256:(e + 1) * 256],
                                         func=ACT.Identity, scale=gb[:, col:col + 1], bias=gb[:, 32 + col:33 + col])

        def RG(x, g, h):
            gn = gnp.tile([P, 256, 4], BF16, name="gn", tag="gn", align_bytes=256)
            dst = gn[:].rearrange("p (c i) t -> p c t i", i=4)
            src = planes[(x, g, h)][:].rearrange("p t (c i) -> p c t i", i=4)
            if (x, g, h) == (1, 3, 1):
                nc.scalar.copy(out=dst, in_=src)
            else:
                nc.vector.tensor_copy(out=dst, in_=src)
            gns[(x, g, h)] = gn

        def QN(x, g, h):
            kp = 4 * h + g
            nc.vector.quantize_mx(out=ncod[x][:, kp * 256:(kp + 1) * 256].bitcast(FP8X4),
                                  scales=nsca[x][:, kp * 256:(kp + 1) * 256],
                                  in_=gns[(x, g, h)][:].rearrange("p b t -> p (b t)"))

        acc2 = {}

        def MM2(x, g, hs):
            for b2 in range(2):
                for cc in range(2):
                    for h in hs:
                        kp = 4 * h + g
                        f = 10 + 2 * g + h
                        first = g == 0 and h == 0
                        if first:
                            acc2[(x, b2, cc)] = bank("acc2")
                        lc = slice(kp * 256 + b2 * 128, kp * 256 + (b2 + 1) * 128)
                        rc = slice(cc * 512, (cc + 1) * 512)
                        nc.tensor.matmul_mx(
                            out=acc2[(x, b2, cc)][:],
                            lhsT=ncod[x][:, lc].bitcast(FP8X4), lhsT_scale=nsca[x][:, lc],
                            rhs=codes[f][:, rc].bitcast(FP8X4), rhs_scale=scales[f][:, rc],
                            start=first, stop=g == 3 and h == 1,
                        )

        def OUT(x, b2s):
            for b2 in b2s:
                for cc in range(2):
                    osb = osp.tile([P, 512], F32, name="osb", tag="osb")
                    r0 = (2 * x + b2) * 128
                    w = 256 if (x, b2, cc) == (1, 1, 1) else 512
                    for c0 in range(0, 512, w):
                        c1 = cc * 512 + c0
                        nc.vector.tensor_tensor(out=osb[:, c0:c0 + w], in0=acc2[(x, b2, cc)][:, c0:c0 + w],
                                                in1=fcb[:, c1:c1 + w], op=ALU.add)
                        nc.sync.dma_start(out=out[r0:r0 + 128, c1:c1 + w], in_=osb[:, c0:c0 + w])

        def due(n, start, count):
            d = n - start
            if d >= 0 and d % 2 == 0 and d // 2 < count:
                return d // 2
            return None

        for pos in range(4):
            for half in range(2):
                T(pos, half)
            if pos < 3:
                for half in range(2):
                    C(pos, half, 1 if pos == 0 else 0)
            if pos == 1:
                for c in range(4):
                    BM(c)
                GT()
            if pos < 2:
                Q(pos, 0, 1)
            if pos in (1, 2):
                S(pos + 2)
        for n in range(N_STEPS):
            x, s = n // 8, n % 8
            for xx in range(2):
                for h in range(2):
                    g = due(n, N0[xx] + RG_LAG[h] + 1, 4)
                    if g is not None:
                        QN(xx, g, h)
            for xx in range(2):
                g = due(n, N0[xx], 4)
                if g is not None:
                    Z(xx, g)
            if n < 16:
                MM1(s, x)
            for h in range(2):
                g = due(n, N0[0] + MM_LAG[h], 4)
                if g is not None:
                    MM2(0, g, (h,))
            g = due(n, N0[1] + MM_LAG[1], 4)
            if g is not None:
                MM2(1, g, (0, 1))
            for pos in range(4, 18):
                for half in range(2):
                    if t_step(pos, half) == n:
                        T(pos, half)
            c = n - N0[0]
            if 0 <= c < 8:
                ZT(0, c // 2, c % 2)
            g = due(n, N0[1], 4)
            if g is not None:
                ZT(1, g, 0)
                ZT(1, g, 1)
            if n == 16:
                TANH(7, 1)
            for pos in range(3, 18):
                for half in range(2):
                    if t_step(pos, half) == n - 1:
                        C(pos, half, 0)
            if 1 <= n <= 15:
                TANH((n - 1) % 8, (n - 1) // 8)
            for xx in range(2):
                c = n - N0[xx] - 1
                if 0 <= c < 8:
                    GB(xx, c // 2, c % 2)
            for xx in range(2):
                for h in range(2):
                    g = due(n, N0[xx] + RG_LAG[h], 4)
                    if g is not None:
                        RG(xx, g, h)
            for xx in range(2):
                for sl in range(8):
                    if n == min(8 * xx + sl + 2, 16):
                        BN(sl, xx)
                if n == LAST_BN[xx]:
                    STATS(xx)
            for pos in range(2, 18):
                if t_step(pos, 0) == t_step(pos, 1):
                    if t_step(pos, 0) == n - 2:
                        Q(pos, 0, 1)
                else:
                    for half in range(2):
                        if t_step(pos, half) == n - 2:
                            Q(pos, half, 2)
            for pos in range(5, 18):
                if t_step(pos, 0) == n + 1:
                    S(pos)
            if n < 16:
                BIAS(s, x)
            if n == N0[0] + MM_LAG[1] + 6:
                OUT(0, (0,))
            if n == N0[1] + MM_LAG[1] + 6:
                OUT(0, (1,))
                OUT(1, (0, 1))
